import numpy as np
import ml_dtypes

BF16 = ml_dtypes.bfloat16


def bf(x):
    return np.asarray(x, np.float32).astype(BF16)


def f32(x):
    return np.asarray(x, np.float32)


def f64(x):
    return np.asarray(x).astype(np.float64)


def striped(idx):
    return np.tile(idx.reshape(-1, 16).T, (8, 1))


B, C, S, HR, K, N, P, D1, D2 = 2, 1024, 256, 128, 32, 4096, 2048, 512, 256


def silu(v):
    return v / (1.0 + np.exp(-v))


def setup_inputs():
    return {
        "pocket": f32(np.random.standard_normal((B, C, S))),
        "lig": f32(np.random.standard_normal((C, N))),
        "w1": bf(np.random.standard_normal((C, D1)) / np.sqrt(C)),
        "b1": f32(0.1 * np.random.standard_normal((D1, 1))),
        "w2": bf(np.random.standard_normal((D1, D2)) / np.sqrt(D1)),
        "b2": f32(0.1 * np.random.standard_normal((D2, 1))),
        "offs": striped(np.concatenate([np.random.permutation(S)[:HR] for _ in range(K)])),
    }


def reference(pocket, lig, w1, b1, w2, b2, offs):
    idx = offs[:16].T.reshape(-1)
    parts = []
    for q in range(B):
        sl = slice(q * P, (q + 1) * P)
        s = f64(pocket)[q][:, idx[sl]] + f64(lig)[:, sl]
        h = silu(f64(w1).T @ s + f64(b1))
        parts.append(silu(f64(w2).T @ h + f64(b2)))
    return np.concatenate(parts, axis=1)

@@ -1,0 +1,106 @@
+import concourse.masks as masks
+import concourse.mybir as mybir
+
+F32 = mybir.dt.float32
+BF16 = mybir.dt.bfloat16
+U16 = mybir.dt.uint16
+ADD = mybir.AluOpType.add
+SILU = mybir.ActivationFunctionType.Silu
+
+P = 128
+B, C, S, N, D1, D2 = 2, 1024, 256, 4096, 512, 256
+PAIRS = N // B
+CB = C // P
+UB = D1 // P
+VB = D2 // P
+CHUNK = 512
+PIECE = S
+NCHUNKS = N // CHUNK
+
+FLOPS = 2 * N * (C * D1 + D1 * D2)
+
+
+def tile_hiddenedgedistancemlp_b_kernel(tc, pocket, lig, w1, b1, w2, b2, offs, out):
+    nc = tc.nc
+    with (
+        tc.tile_pool(name="held", bufs=1) as held,
+        tc.tile_pool(name="lig_ring", bufs=3) as lig_ring,
+        tc.tile_pool(name="sum_ring", bufs=4) as sum_ring,
+        tc.tile_pool(name="act_ring", bufs=3) as act_ring,
+        tc.tile_pool(name="out_ring", bufs=4) as out_ring,
+        tc.psum_pool(name="psum_setup", bufs=1) as psum_setup,
+        tc.psum_pool(name="psum1", bufs=5) as psum1,
+        tc.psum_pool(name="psum2", bufs=2) as psum2,
+    ):
+        offsets = held.tile([P, N // 16], U16, name="offsets")
+        nc.sync.dma_start(offsets[:], offs)
+
+        windows = [[held.tile([P, S], F32, name=f"window{q}_{k}") for k in range(CB)] for q in range(B)]
+        w1_sb = held.tile([P, CB, D1], BF16, name="w1_sb")
+        w2_sb = held.tile([P, UB, D2], BF16, name="w2_sb")
+
+        identity = held.tile([P, P], F32, name="identity")
+        masks.make_identity(nc, identity[:])
+        bias_rows = held.tile([P, P], F32, name="bias_rows")
+        nc.gpsimd.memset(bias_rows[:], 0.0)
+        bias_cols = held.tile([P, UB + VB], F32, name="bias_cols")
+
+        for c in range(NCHUNKS):
+            q = c * CHUNK // PAIRS
+            cols = slice(c * CHUNK, (c + 1) * CHUNK)
+
+            lig_sb = lig_ring.tile([P, CB, CHUNK], F32, name="lig_sb")
+            for k in range(CB):
+                rows = slice(k * P, (k + 1) * P)
+                if c * CHUNK % PAIRS == 0:
+                    nc.sync.dma_start(windows[q][k][:], pocket[q, rows, :])
+                nc.sync.dma_start(lig_sb[:, k, :], lig[rows, cols])
+                if c == 0:
+                    nc.sync.dma_start(w1_sb[:, k, :], w1[rows, :])
+            if c == 0:
+                nc.sync.dma_start(w2_sb[:], w2.rearrange("(u p) v -> p u v", p=P))
+                nc.sync.dma_start(bias_rows[0:UB, :], b1.rearrange("(m p) o -> m (p o)", p=P))
+                nc.sync.dma_start(bias_rows[UB : UB + VB, :], b2.rearrange("(m p) o -> m (p o)", p=P))
+                bias_ps = psum_setup.tile([P, P], F32, name="bias_ps")
+                nc.tensor.transpose(bias_ps[:], bias_rows[:], identity[:])
+                nc.vector.tensor_copy(bias_cols[:], bias_ps[:, 0 : UB + VB])
+
+            s_bf = act_ring.tile([P, CB, CHUNK], BF16, name="s_bf")
+            h_ps = [psum1.tile([P, CHUNK], F32, name=f"h_ps{m}", tag="h_ps") for m in range(UB)]
+            for k in range(CB):
+                s_f32 = sum_ring.tile([P, CHUNK], F32, name="s_f32")
+                for piece in range(CHUNK // PIECE):
+                    first = c * CHUNK + piece * PIECE
+                    part = slice(piece * PIECE, (piece + 1) * PIECE)
+                    nc.vector.tensor_tensor(
+                        s_f32[:, part],
+                        windows[q][k][:].indirect(offsets[:, first // 16 : (first + PIECE) // 16]),
+                        lig_sb[:, k, part],
+                        ADD,
+                    )
+                nc.scalar.copy(s_bf[:, k, :], s_f32[:])
+                for m in range(UB):
+                    nc.tensor.matmul(
+                        h_ps[m][:],
+                        w1_sb[:, k, m * P : (m + 1) * P],
+                        s_bf[:, k, :],
+                        start=(k == 0),
+                        stop=(k == CB - 1),
+                    )
+            h_bf = act_ring.tile([P, UB, CHUNK], BF16, name="h_bf")
+            for m in range(UB):
+                nc.scalar.activation(h_bf[:, m, :], h_ps[m][:], SILU, bias=bias_cols[:, m : m + 1])
+
+            for v in range(VB):
+                o_ps = psum2.tile([P, CHUNK], F32, name="o_ps")
+                for u in range(UB):
+                    nc.tensor.matmul(
+                        o_ps[:],
+                        w2_sb[:, u, v * P : (v + 1) * P],
+                        h_bf[:, u, :],
+                        start=(u == 0),
+                        stop=(u == UB - 1),
+                    )
+                o_sb = out_ring.tile([P, CHUNK], F32, name="o_sb")
+                nc.scalar.activation(o_sb[:], o_ps[:], SILU, bias=bias_cols[:, UB + v : UB + v + 1])
+                nc.sync.dma_start(out[v * P : (v + 1) * P, cols], o_sb[:])

@@ -16,6 +16,8 @@ VB = D2 // P
 CHUNK = 512
 PIECE = S
 NCHUNKS = N // CHUNK
+LOAD_AHEAD = 2
+SUM_AHEAD = 2
 
 FLOPS = 2 * N * (C * D1 + D1 * D2)
 
@@ -24,12 +26,11 @@ def tile_hiddenedgedistancemlp_b_kernel(tc, pocket, lig, w1, b1, w2, b2, offs, o
     nc = tc.nc
     with (
         tc.tile_pool(name="held", bufs=1) as held,
-        tc.tile_pool(name="lig_ring", bufs=3) as lig_ring,
+        tc.tile_pool(name="lig_ring", bufs=LOAD_AHEAD + 1) as lig_ring,
         tc.tile_pool(name="sum_ring", bufs=4) as sum_ring,
         tc.tile_pool(name="act_ring", bufs=3) as act_ring,
         tc.tile_pool(name="out_ring", bufs=4) as out_ring,
-        tc.psum_pool(name="psum_setup", bufs=1) as psum_setup,
-        tc.psum_pool(name="psum1", bufs=5) as psum1,
+        tc.psum_pool(name="psum1", bufs=6) as psum1,
         tc.psum_pool(name="psum2", bufs=2) as psum2,
     ):
         offsets = held.tile([P, N // 16], U16, name="offsets")
@@ -38,69 +39,95 @@ def tile_hiddenedgedistancemlp_b_kernel(tc, pocket, lig, w1, b1, w2, b2, offs, o
         windows = [[held.tile([P, S], F32, name=f"window{q}_{k}") for k in range(CB)] for q in range(B)]
         w1_sb = held.tile([P, CB, D1], BF16, name="w1_sb")
         w2_sb = held.tile([P, UB, D2], BF16, name="w2_sb")
+        lig_sb, s_bf, h_ps, h_bf = {}, {}, {}, {}
 
         identity = held.tile([P, P], F32, name="identity")
         masks.make_identity(nc, identity[:])
         bias_rows = held.tile([P, P], F32, name="bias_rows")
         nc.gpsimd.memset(bias_rows[:], 0.0)
+        nc.scalar.dma_start(bias_rows[0:UB, :], b1.rearrange("(m p) o -> m (p o)", p=P))
+        nc.scalar.dma_start(bias_rows[UB : UB + VB, :], b2.rearrange("(m p) o -> m (p o)", p=P))
+        bias_ps = psum2.tile([P, P], F32, name="bias_ps", tag="o_ps")
+        nc.tensor.transpose(bias_ps[:], bias_rows[:], identity[:])
         bias_cols = held.tile([P, UB + VB], F32, name="bias_cols")
+        nc.scalar.copy(bias_cols[:], bias_ps[:, 0 : UB + VB])
 
-        for c in range(NCHUNKS):
-            q = c * CHUNK // PAIRS
-            cols = slice(c * CHUNK, (c + 1) * CHUNK)
+        def load_block(c, k):
+            rows = slice(k * P, (k + 1) * P)
+            if k == 0:
+                lig_sb[c] = lig_ring.tile([P, CB, CHUNK], F32, name="lig_sb")
+            if c * CHUNK % PAIRS == 0:
+                nc.sync.dma_start(windows[c * CHUNK // PAIRS][k][:], pocket[c * CHUNK // PAIRS, rows, :])
+            nc.sync.dma_start(lig_sb[c][:, k, :], lig[rows, c * CHUNK : (c + 1) * CHUNK])
 
-            lig_sb = lig_ring.tile([P, CB, CHUNK], F32, name="lig_sb")
-            for k in range(CB):
-                rows = slice(k * P, (k + 1) * P)
-                if c * CHUNK % PAIRS == 0:
-                    nc.sync.dma_start(windows[q][k][:], pocket[q, rows, :])
-                nc.sync.dma_start(lig_sb[:, k, :], lig[rows, cols])
-                if c == 0:
-                    nc.sync.dma_start(w1_sb[:, k, :], w1[rows, :])
-            if c == 0:
-                nc.sync.dma_start(w2_sb[:], w2.rearrange("(u p) v -> p u v", p=P))
-                nc.sync.dma_start(bias_rows[0:UB, :], b1.rearrange("(m p) o -> m (p o)", p=P))
-                nc.sync.dma_start(bias_rows[UB : UB + VB, :], b2.rearrange("(m p) o -> m (p o)", p=P))
-                bias_ps = psum_setup.tile([P, P], F32, name="bias_ps")
-                nc.tensor.transpose(bias_ps[:], bias_rows[:], identity[:])
-                nc.vector.tensor_copy(bias_cols[:], bias_ps[:, 0 : UB + VB])
+        def sum_block(c, k):
+            if k == 0:
+                s_bf[c] = act_ring.tile([P, CB, CHUNK], BF16, name="s_bf")
+            s_f32 = sum_ring.tile([P, CHUNK], F32, name="s_f32")
+            for piece in range(CHUNK // PIECE):
+                first = c * CHUNK + piece * PIECE
+                part = slice(piece * PIECE, (piece + 1) * PIECE)
+                nc.vector.tensor_tensor(
+                    s_f32[:, part],
+                    windows[c * CHUNK // PAIRS][k][:].indirect(offsets[:, first // 16 : (first + PIECE) // 16]),
+                    lig_sb[c][:, k, part],
+                    ADD,
+                )
+            nc.scalar.copy(s_bf[c][:, k, :], s_f32[:])
 
-            s_bf = act_ring.tile([P, CB, CHUNK], BF16, name="s_bf")
-            h_ps = [psum1.tile([P, CHUNK], F32, name=f"h_ps{m}", tag="h_ps") for m in range(UB)]
-            for k in range(CB):
-                s_f32 = sum_ring.tile([P, CHUNK], F32, name="s_f32")
-                for piece in range(CHUNK // PIECE):
-                    first = c * CHUNK + piece * PIECE
-                    part = slice(piece * PIECE, (piece + 1) * PIECE)
-                    nc.vector.tensor_tensor(
-                        s_f32[:, part],
-                        windows[q][k][:].indirect(offsets[:, first // 16 : (first + PIECE) // 16]),
-                        lig_sb[:, k, part],
-                        ADD,
-                    )
-                nc.scalar.copy(s_bf[:, k, :], s_f32[:])
-                for m in range(UB):
-                    nc.tensor.matmul(
-                        h_ps[m][:],
-                        w1_sb[:, k, m * P : (m + 1) * P],
-                        s_bf[:, k, :],
-                        start=(k == 0),
-                        stop=(k == CB - 1),
-                    )
-            h_bf = act_ring.tile([P, UB, CHUNK], BF16, name="h_bf")
+        def layer1_block(c, k):
+            if k == 0:
+                h_ps[c] = [psum1.tile([P, CHUNK], F32, name=f"h_ps{m}", tag="h_ps") for m in range(UB)]
             for m in range(UB):
-                nc.scalar.activation(h_bf[:, m, :], h_ps[m][:], SILU, bias=bias_cols[:, m : m + 1])
+                nc.tensor.matmul(
+                    h_ps[c][m][:],
+                    w1_sb[:, k, m * P : (m + 1) * P],
+                    s_bf[c][:, k, :],
+                    start=(k == 0),
+                    stop=(k == CB - 1),
+                )
 
+        def layer1_silu(c):
+            h_bf[c] = act_ring.tile([P, UB, CHUNK], BF16, name="h_bf")
+            for m in range(UB):
+                nc.scalar.activation(h_bf[c][:, m, :], h_ps[c][m][:], SILU, bias=bias_cols[:, m : m + 1])
+
+        def layer2(c):
+            o_ps = [psum2.tile([P, CHUNK], F32, name=f"o_ps{v}", tag="o_ps") for v in range(VB)]
             for v in range(VB):
-                o_ps = psum2.tile([P, CHUNK], F32, name="o_ps")
                 for u in range(UB):
                     nc.tensor.matmul(
-                        o_ps[:],
+                        o_ps[v][:],
                         w2_sb[:, u, v * P : (v + 1) * P],
-                        h_bf[:, u, :],
+                        h_bf[c][:, u, :],
                         start=(u == 0),
                         stop=(u == UB - 1),
                     )
+            for v in range(VB):
                 o_sb = out_ring.tile([P, CHUNK], F32, name="o_sb")
-                nc.scalar.activation(o_sb[:], o_ps[:], SILU, bias=bias_cols[:, UB + v : UB + v + 1])
-                nc.sync.dma_start(out[v * P : (v + 1) * P, cols], o_sb[:])
+                nc.scalar.activation(o_sb[:], o_ps[v][:], SILU, bias=bias_cols[:, UB + v : UB + v + 1])
+                nc.sync.dma_start(out[v * P : (v + 1) * P, c * CHUNK : (c + 1) * CHUNK], o_sb[:])
+
+        for k in range(CB):
+            load_block(0, k)
+            nc.sync.dma_start(w1_sb[:, k, :], w1[k * P : (k + 1) * P, :])
+        nc.sync.dma_start(w2_sb[:], w2.rearrange("(u p) v -> p u v", p=P))
+        for c in range(1, LOAD_AHEAD):
+            for k in range(CB):
+                load_block(c, k)
+
+        blocks = [(c, k) for c in range(NCHUNKS) for k in range(CB)]
+        for step in range(len(blocks) + SUM_AHEAD):
+            if step < len(blocks):
+                c, k = blocks[step]
+                if c + LOAD_AHEAD < NCHUNKS:
+                    load_block(c + LOAD_AHEAD, k)
+                sum_block(c, k)
+            if step >= SUM_AHEAD:
+                c, k = blocks[step - SUM_AHEAD]
+                layer1_block(c, k)
+                if k == CB - 1:
+                    layer1_silu(c)
+                    if c > 0:
+                        layer2(c - 1)
+        layer2(NCHUNKS - 1)

@@ -18,6 +18,7 @@ PIECE = S
 NCHUNKS = N // CHUNK
 LOAD_AHEAD = 2
 SUM_AHEAD = 2
+SUM_LEAD = 4
 
 FLOPS = 2 * N * (C * D1 + D1 * D2)
 
@@ -28,13 +29,18 @@ def tile_hiddenedgedistancemlp_b_kernel(tc, pocket, lig, w1, b1, w2, b2, offs, o
         tc.tile_pool(name="held", bufs=1) as held,
         tc.tile_pool(name="lig_ring", bufs=LOAD_AHEAD + 1) as lig_ring,
         tc.tile_pool(name="sum_ring", bufs=4) as sum_ring,
-        tc.tile_pool(name="act_ring", bufs=3) as act_ring,
+        tc.tile_pool(name="s_ring", bufs=SUM_LEAD) as s_ring,
+        tc.tile_pool(name="h_ring", bufs=2) as h_ring,
         tc.tile_pool(name="out_ring", bufs=4) as out_ring,
         tc.psum_pool(name="psum1", bufs=6) as psum1,
         tc.psum_pool(name="psum2", bufs=2) as psum2,
     ):
         offsets = held.tile([P, N // 16], U16, name="offsets")
         nc.sync.dma_start(offsets[:], offs)
+
+        warm = held.tile([P, 1], F32, name="warm")
+        nc.gpsimd.memset(warm[:], 0.0)
+        nc.scalar.activation(warm[:], warm[:], SILU)
 
         windows = [[held.tile([P, S], F32, name=f"window{q}_{k}") for k in range(CB)] for q in range(B)]
         w1_sb = held.tile([P, CB, D1], BF16, name="w1_sb")
@@ -61,8 +67,7 @@ def tile_hiddenedgedistancemlp_b_kernel(tc, pocket, lig, w1, b1, w2, b2, offs, o
             nc.sync.dma_start(lig_sb[c][:, k, :], lig[rows, c * CHUNK : (c + 1) * CHUNK])
 
         def sum_block(c, k):
-            if k == 0:
-                s_bf[c] = act_ring.tile([P, CB, CHUNK], BF16, name="s_bf")
+            s_bf[c, k] = s_ring.tile([P, CHUNK], BF16, name="s_bf")
             s_f32 = sum_ring.tile([P, CHUNK], F32, name="s_f32")
             for piece in range(CHUNK // PIECE):
                 first = c * CHUNK + piece * PIECE
@@ -73,7 +78,7 @@ def tile_hiddenedgedistancemlp_b_kernel(tc, pocket, lig, w1, b1, w2, b2, offs, o
                     lig_sb[c][:, k, part],
                     ADD,
                 )
-            nc.scalar.copy(s_bf[c][:, k, :], s_f32[:])
+            nc.scalar.copy(s_bf[c, k][:], s_f32[:])
 
         def layer1_block(c, k):
             if k == 0:
@@ -82,13 +87,13 @@ def tile_hiddenedgedistancemlp_b_kernel(tc, pocket, lig, w1, b1, w2, b2, offs, o
                 nc.tensor.matmul(
                     h_ps[c][m][:],
                     w1_sb[:, k, m * P : (m + 1) * P],
-                    s_bf[c][:, k, :],
+                    s_bf[c, k][:],
                     start=(k == 0),
                     stop=(k == CB - 1),
                 )
 
         def layer1_silu(c):
-            h_bf[c] = act_ring.tile([P, UB, CHUNK], BF16, name="h_bf")
+            h_bf[c] = h_ring.tile([P, UB, CHUNK], BF16, name="h_bf")
             for m in range(UB):
                 nc.scalar.activation(h_bf[c][:, m, :], h_ps[c][m][:], SILU, bias=bias_cols[:, m : m + 1])
 

@@ -14,11 +14,9 @@ CB = C // P
 UB = D1 // P
 VB = D2 // P
 CHUNK = 512
-PIECE = S
 NCHUNKS = N // CHUNK
+PIECE = S
 LOAD_AHEAD = 2
-SUM_AHEAD = 2
-SUM_LEAD = 4
 
 FLOPS = 2 * N * (C * D1 + D1 * D2)
 
@@ -29,11 +27,11 @@ def tile_hiddenedgedistancemlp_b_kernel(tc, pocket, lig, w1, b1, w2, b2, offs, o
         tc.tile_pool(name="held", bufs=1) as held,
         tc.tile_pool(name="lig_ring", bufs=LOAD_AHEAD + 1) as lig_ring,
         tc.tile_pool(name="sum_ring", bufs=4) as sum_ring,
-        tc.tile_pool(name="s_ring", bufs=SUM_LEAD) as s_ring,
-        tc.tile_pool(name="h_ring", bufs=2) as h_ring,
-        tc.tile_pool(name="out_ring", bufs=4) as out_ring,
-        tc.psum_pool(name="psum1", bufs=6) as psum1,
-        tc.psum_pool(name="psum2", bufs=2) as psum2,
+        tc.tile_pool(name="rounded_ring", bufs=3) as rounded_ring,
+        tc.tile_pool(name="hidden_ring", bufs=2) as hidden_ring,
+        tc.tile_pool(name="out_ring", bufs=2 * VB) as out_ring,
+        tc.psum_pool(name="psum1", bufs=8 - VB) as psum1,
+        tc.psum_pool(name="psum2", bufs=VB) as psum2,
     ):
         offsets = held.tile([P, N // 16], U16, name="offsets")
         nc.sync.dma_start(offsets[:], offs)
@@ -42,21 +40,21 @@ def tile_hiddenedgedistancemlp_b_kernel(tc, pocket, lig, w1, b1, w2, b2, offs, o
         nc.gpsimd.memset(warm[:], 0.0)
         nc.scalar.activation(warm[:], warm[:], SILU)
 
-        windows = [[held.tile([P, S], F32, name=f"window{q}_{k}") for k in range(CB)] for q in range(B)]
-        w1_sb = held.tile([P, CB, D1], BF16, name="w1_sb")
-        w2_sb = held.tile([P, UB, D2], BF16, name="w2_sb")
-        lig_sb, s_bf, h_ps, h_bf = {}, {}, {}, {}
-
         identity = held.tile([P, P], F32, name="identity")
         masks.make_identity(nc, identity[:])
         bias_rows = held.tile([P, P], F32, name="bias_rows")
         nc.gpsimd.memset(bias_rows[:], 0.0)
         nc.scalar.dma_start(bias_rows[0:UB, :], b1.rearrange("(m p) o -> m (p o)", p=P))
-        nc.scalar.dma_start(bias_rows[UB : UB + VB, :], b2.rearrange("(m p) o -> m (p o)", p=P))
+        nc.scalar.dma_start(bias_rows[UB : UB + VB, :], b2.rearrange("(v p) o -> v (p o)", p=P))
         bias_ps = psum2.tile([P, P], F32, name="bias_ps", tag="o_ps")
         nc.tensor.transpose(bias_ps[:], bias_rows[:], identity[:])
         bias_cols = held.tile([P, UB + VB], F32, name="bias_cols")
         nc.scalar.copy(bias_cols[:], bias_ps[:, 0 : UB + VB])
+
+        windows = [[held.tile([P, S], F32, name=f"window{q}_{k}") for k in range(CB)] for q in range(B)]
+        w1_sb = held.tile([P, CB, D1], BF16, name="w1_sb")
+        w2_sb = held.tile([P, UB, D2], BF16, name="w2_sb")
+        lig_sb = {}
 
         def load_block(c, k):
             rows = slice(k * P, (k + 1) * P)
@@ -66,53 +64,6 @@ def tile_hiddenedgedistancemlp_b_kernel(tc, pocket, lig, w1, b1, w2, b2, offs, o
                 nc.sync.dma_start(windows[c * CHUNK // PAIRS][k][:], pocket[c * CHUNK // PAIRS, rows, :])
             nc.sync.dma_start(lig_sb[c][:, k, :], lig[rows, c * CHUNK : (c + 1) * CHUNK])
 
-        def sum_block(c, k):
-            s_bf[c, k] = s_ring.tile([P, CHUNK], BF16, name="s_bf")
-            s_f32 = sum_ring.tile([P, CHUNK], F32, name="s_f32")
-            for piece in range(CHUNK // PIECE):
-                first = c * CHUNK + piece * PIECE
-                part = slice(piece * PIECE, (piece + 1) * PIECE)
-                nc.vector.tensor_tensor(
-                    s_f32[:, part],
-                    windows[c * CHUNK // PAIRS][k][:].indirect(offsets[:, first // 16 : (first + PIECE) // 16]),
-                    lig_sb[c][:, k, part],
-                    ADD,
-                )
-            nc.scalar.copy(s_bf[c, k][:], s_f32[:])
-
-        def layer1_block(c, k):
-            if k == 0:
-                h_ps[c] = [psum1.tile([P, CHUNK], F32, name=f"h_ps{m}", tag="h_ps") for m in range(UB)]
-            for m in range(UB):
-                nc.tensor.matmul(
-                    h_ps[c][m][:],
-                    w1_sb[:, k, m * P : (m + 1) * P],
-                    s_bf[c, k][:],
-                    start=(k == 0),
-                    stop=(k == CB - 1),
-                )
-
-        def layer1_silu(c):
-            h_bf[c] = h_ring.tile([P, UB, CHUNK], BF16, name="h_bf")
-            for m in range(UB):
-                nc.scalar.activation(h_bf[c][:, m, :], h_ps[c][m][:], SILU, bias=bias_cols[:, m : m + 1])
-
-        def layer2(c):
-            o_ps = [psum2.tile([P, CHUNK], F32, name=f"o_ps{v}", tag="o_ps") for v in range(VB)]
-            for v in range(VB):
-                for u in range(UB):
-                    nc.tensor.matmul(
-                        o_ps[v][:],
-                        w2_sb[:, u, v * P : (v + 1) * P],
-                        h_bf[c][:, u, :],
-                        start=(u == 0),
-                        stop=(u == UB - 1),
-                    )
-            for v in range(VB):
-                o_sb = out_ring.tile([P, CHUNK], F32, name="o_sb")
-                nc.scalar.activation(o_sb[:], o_ps[v][:], SILU, bias=bias_cols[:, UB + v : UB + v + 1])
-                nc.sync.dma_start(out[v * P : (v + 1) * P, c * CHUNK : (c + 1) * CHUNK], o_sb[:])
-
         for k in range(CB):
             load_block(0, k)
             nc.sync.dma_start(w1_sb[:, k, :], w1[k * P : (k + 1) * P, :])
@@ -121,18 +72,47 @@ def tile_hiddenedgedistancemlp_b_kernel(tc, pocket, lig, w1, b1, w2, b2, offs, o
             for k in range(CB):
                 load_block(c, k)
 
-        blocks = [(c, k) for c in range(NCHUNKS) for k in range(CB)]
-        for step in range(len(blocks) + SUM_AHEAD):
-            if step < len(blocks):
-                c, k = blocks[step]
+        for c in range(NCHUNKS):
+            q = c * CHUNK // PAIRS
+
+            h_ps = [psum1.tile([P, CHUNK], F32, name=f"h_ps{m}", tag="h_ps") for m in range(UB)]
+            for k in range(CB):
                 if c + LOAD_AHEAD < NCHUNKS:
                     load_block(c + LOAD_AHEAD, k)
-                sum_block(c, k)
-            if step >= SUM_AHEAD:
-                c, k = blocks[step - SUM_AHEAD]
-                layer1_block(c, k)
-                if k == CB - 1:
-                    layer1_silu(c)
-                    if c > 0:
-                        layer2(c - 1)
-        layer2(NCHUNKS - 1)
+                s_f32 = sum_ring.tile([P, CHUNK], F32, name="s_f32")
+                for piece in range(CHUNK // PIECE):
+                    first = c * CHUNK + piece * PIECE
+                    part = slice(piece * PIECE, (piece + 1) * PIECE)
+                    nc.vector.tensor_tensor(
+                        s_f32[:, part],
+                        windows[q][k][:].indirect(offsets[:, first // 16 : (first + PIECE) // 16]),
+                        lig_sb[c][:, k, part],
+                        ADD,
+                    )
+                s_bf = rounded_ring.tile([P, CHUNK], BF16, name="s_bf")
+                nc.scalar.copy(s_bf[:], s_f32[:])
+                for m in range(UB):
+                    nc.tensor.matmul(
+                        h_ps[m][:],
+                        w1_sb[:, k, m * P : (m + 1) * P],
+                        s_bf[:],
+                        start=(k == 0),
+                        stop=(k == CB - 1),
+                    )
+            h_bf = hidden_ring.tile([P, UB, CHUNK], BF16, name="h_bf")
+            for m in range(UB):
+                nc.scalar.activation(h_bf[:, m, :], h_ps[m][:], SILU, bias=bias_cols[:, m : m + 1])
+
+            for v in range(VB):
+                o_ps = psum2.tile([P, CHUNK], F32, name="o_ps")
+                for u in range(UB):
+                    nc.tensor.matmul(
+                        o_ps[:],
+                        w2_sb[:, u, v * P : (v + 1) * P],
+                        h_bf[:, u, :],
+                        start=(u == 0),
+                        stop=(u == UB - 1),
+                    )
+                o_sb = out_ring.tile([P, CHUNK], F32, name="o_sb")
+                nc.scalar.activation(o_sb[:], o_ps[:], SILU, bias=bias_cols[:, UB + v : UB + v + 1])
+                nc.sync.dma_start(out[v * P : (v + 1) * P, c * CHUNK : (c + 1) * CHUNK], o_sb[:])

@@ -17,6 +17,7 @@ CHUNK = 512
 NCHUNKS = N // CHUNK
 PIECE = S
 LOAD_AHEAD = 2
+CLOSING = 2
 
 FLOPS = 2 * N * (C * D1 + D1 * D2)
 
@@ -76,27 +77,42 @@ def tile_hiddenedgedistancemlp_b_kernel(tc, pocket, lig, w1, b1, w2, b2, offs, o
             q = c * CHUNK // PAIRS
 
             h_ps = [psum1.tile([P, CHUNK], F32, name=f"h_ps{m}", tag="h_ps") for m in range(UB)]
+            step = PIECE if c == 0 else CHUNK
+            kept = 0 if c == 0 else CLOSING
+            closing = []
             for k in range(CB):
                 if c + LOAD_AHEAD < NCHUNKS:
                     load_block(c + LOAD_AHEAD, k)
-                s_f32 = sum_ring.tile([P, CHUNK], F32, name="s_f32")
-                for piece in range(CHUNK // PIECE):
-                    first = c * CHUNK + piece * PIECE
-                    part = slice(piece * PIECE, (piece + 1) * PIECE)
-                    nc.vector.tensor_tensor(
-                        s_f32[:, part],
-                        windows[q][k][:].indirect(offsets[:, first // 16 : (first + PIECE) // 16]),
-                        lig_sb[c][:, k, part],
-                        ADD,
-                    )
-                s_bf = rounded_ring.tile([P, CHUNK], BF16, name="s_bf")
-                nc.scalar.copy(s_bf[:], s_f32[:])
-                for m in range(UB):
+                for at in range(0, CHUNK, step):
+                    s_f32 = sum_ring.tile([P, step], F32, name="s_f32")
+                    for piece in range(step // PIECE):
+                        first = c * CHUNK + at + piece * PIECE
+                        nc.vector.tensor_tensor(
+                            s_f32[:, piece * PIECE : (piece + 1) * PIECE],
+                            windows[q][k][:].indirect(offsets[:, first // 16 : (first + PIECE) // 16]),
+                            lig_sb[c][:, k, at + piece * PIECE : at + (piece + 1) * PIECE],
+                            ADD,
+                        )
+                    s_bf = rounded_ring.tile([P, step], BF16, name="s_bf")
+                    nc.scalar.copy(s_bf[:], s_f32[:])
+                    if k >= CB - kept:
+                        closing.append((k, s_bf))
+                        continue
+                    for m in range(UB):
+                        nc.tensor.matmul(
+                            h_ps[m][:, at : at + step],
+                            w1_sb[:, k, m * P : (m + 1) * P],
+                            s_bf[:],
+                            start=(k == 0 and at == 0),
+                            stop=(k == CB - 1 and at + step == CHUNK),
+                        )
+            for m in range(UB):
+                for k, s_bf in closing:
                     nc.tensor.matmul(
                         h_ps[m][:],
                         w1_sb[:, k, m * P : (m + 1) * P],
                         s_bf[:],
-                        start=(k == 0),
+                        start=False,
                         stop=(k == CB - 1),
                     )
             h_bf = hidden_ring.tile([P, UB, CHUNK], BF16, name="h_bf")

@@ -115,20 +115,29 @@ def tile_hiddenedgedistancemlp_b_kernel(tc, pocket, lig, w1, b1, w2, b2, offs, o
                         start=False,
                         stop=(k == CB - 1),
                     )
+            last = c == NCHUNKS - 1
+            span = CHUNK // 2 if last else CHUNK
             h_bf = hidden_ring.tile([P, UB, CHUNK], BF16, name="h_bf")
-            for m in range(UB):
-                nc.scalar.activation(h_bf[:, m, :], h_ps[m][:], SILU, bias=bias_cols[:, m : m + 1])
-
-            for v in range(VB):
-                o_ps = psum2.tile([P, CHUNK], F32, name="o_ps")
-                for u in range(UB):
-                    nc.tensor.matmul(
-                        o_ps[:],
-                        w2_sb[:, u, v * P : (v + 1) * P],
-                        h_bf[:, u, :],
-                        start=(u == 0),
-                        stop=(u == UB - 1),
+            for at in range(0, CHUNK, span):
+                for m in range(UB):
+                    nc.scalar.activation(
+                        h_bf[:, m, at : at + span], h_ps[m][:, at : at + span], SILU, bias=bias_cols[:, m : m + 1]
                     )
-                o_sb = out_ring.tile([P, CHUNK], F32, name="o_sb")
-                nc.scalar.activation(o_sb[:], o_ps[:], SILU, bias=bias_cols[:, UB + v : UB + v + 1])
-                nc.sync.dma_start(out[v * P : (v + 1) * P, c * CHUNK : (c + 1) * CHUNK], o_sb[:])
+
+            for at in range(0, CHUNK, span):
+                for v in range(VB):
+                    if last:
+                        o_ps = psum1.tile([P, span], F32, name="o_ps_last", tag="h_ps")
+                    else:
+                        o_ps = psum2.tile([P, span], F32, name="o_ps")
+                    for u in range(UB):
+                        nc.tensor.matmul(
+                            o_ps[:],
+                            w2_sb[:, u, v * P : (v + 1) * P],
+                            h_bf[:, u, at : at + span],
+                            start=(u == 0),
+                            stop=(u == UB - 1),
+                        )
+                    o_sb = out_ring.tile([P, span], F32, name="o_sb")
+                    nc.scalar.activation(o_sb[:], o_ps[:], SILU, bias=bias_cols[:, UB + v : UB + v + 1])
+                    nc.sync.dma_start(out[v * P : (v + 1) * P, c * CHUNK + at : c * CHUNK + at + span], o_sb[:])

@@ -16,7 +16,7 @@ VB = D2 // P
 CHUNK = 512
 NCHUNKS = N // CHUNK
 PIECE = S
-LOAD_AHEAD = 2
+LOAD_AHEAD = 3
 CLOSING = 2
 
 FLOPS = 2 * N * (C * D1 + D1 * D2)
@@ -27,7 +27,7 @@ def tile_hiddenedgedistancemlp_b_kernel(tc, pocket, lig, w1, b1, w2, b2, offs, o
     with (
         tc.tile_pool(name="held", bufs=1) as held,
         tc.tile_pool(name="lig_ring", bufs=LOAD_AHEAD + 1) as lig_ring,
-        tc.tile_pool(name="sum_ring", bufs=4) as sum_ring,
+        tc.tile_pool(name="sum_ring", bufs=6) as sum_ring,
         tc.tile_pool(name="rounded_ring", bufs=3) as rounded_ring,
         tc.tile_pool(name="hidden_ring", bufs=2) as hidden_ring,
         tc.tile_pool(name="out_ring", bufs=2 * VB) as out_ring,

@@ -18,6 +18,7 @@ NCHUNKS = N // CHUNK
 PIECE = S
 LOAD_AHEAD = 3
 CLOSING = 2
+DEFER = 2
 
 FLOPS = 2 * N * (C * D1 + D1 * D2)
 
@@ -73,6 +74,28 @@ def tile_hiddenedgedistancemlp_b_kernel(tc, pocket, lig, w1, b1, w2, b2, offs, o
             for k in range(CB):
                 load_block(c, k)
 
+        def layer2(c, h_bf):
+            last = c == NCHUNKS - 1
+            span = CHUNK // 2 if last else CHUNK
+            for at in range(0, CHUNK, span):
+                for v in range(VB):
+                    if last:
+                        o_ps = psum1.tile([P, span], F32, name="o_ps_last", tag="h_ps")
+                    else:
+                        o_ps = psum2.tile([P, span], F32, name="o_ps")
+                    for u in range(UB):
+                        nc.tensor.matmul(
+                            o_ps[:],
+                            w2_sb[:, u, v * P : (v + 1) * P],
+                            h_bf[:, u, at : at + span],
+                            start=(u == 0),
+                            stop=(u == UB - 1),
+                        )
+                    o_sb = out_ring.tile([P, span], F32, name="o_sb")
+                    nc.scalar.activation(o_sb[:], o_ps[:], SILU, bias=bias_cols[:, UB + v : UB + v + 1])
+                    nc.sync.dma_start(out[v * P : (v + 1) * P, c * CHUNK + at : c * CHUNK + at + span], o_sb[:])
+
+        waiting = None
         for c in range(NCHUNKS):
             q = c * CHUNK // PAIRS
 
@@ -81,6 +104,8 @@ def tile_hiddenedgedistancemlp_b_kernel(tc, pocket, lig, w1, b1, w2, b2, offs, o
             kept = 0 if c == 0 else CLOSING
             closing = []
             for k in range(CB):
+                if k == DEFER and waiting is not None:
+                    layer2(*waiting)
                 if c + LOAD_AHEAD < NCHUNKS:
                     load_block(c + LOAD_AHEAD, k)
                 for at in range(0, CHUNK, step):
@@ -123,21 +148,5 @@ def tile_hiddenedgedistancemlp_b_kernel(tc, pocket, lig, w1, b1, w2, b2, offs, o
                     nc.scalar.activation(
                         h_bf[:, m, at : at + span], h_ps[m][:, at : at + span], SILU, bias=bias_cols[:, m : m + 1]
                     )
-
-            for at in range(0, CHUNK, span):
-                for v in range(VB):
-                    if last:
-                        o_ps = psum1.tile([P, span], F32, name="o_ps_last", tag="h_ps")
-                    else:
-                        o_ps = psum2.tile([P, span], F32, name="o_ps")
-                    for u in range(UB):
-                        nc.tensor.matmul(
-                            o_ps[:],
-                            w2_sb[:, u, v * P : (v + 1) * P],
-                            h_bf[:, u, at : at + span],
-                            start=(u == 0),
-                            stop=(u == UB - 1),
-                        )
-                    o_sb = out_ring.tile([P, span], F32, name="o_sb")
-                    nc.scalar.activation(o_sb[:], o_ps[:], SILU, bias=bias_cols[:, UB + v : UB + v + 1])
-                    nc.sync.dma_start(out[v * P : (v + 1) * P, c * CHUNK + at : c * CHUNK + at + span], o_sb[:])
+            waiting = (c, h_bf)
+        layer2(*waiting)

@@ -69,9 +69,10 @@ def tile_hiddenedgedistancemlp_b_kernel(tc, pocket, lig, w1, b1, w2, b2, offs, o
         for k in range(CB):
             load_block(0, k)
             nc.sync.dma_start(w1_sb[:, k, :], w1[k * P : (k + 1) * P, :])
-        nc.sync.dma_start(w2_sb[:], w2.rearrange("(u p) v -> p u v", p=P))
         for c in range(1, LOAD_AHEAD):
             for k in range(CB):
+                if c == 1 and k == DEFER:
+                    nc.sync.dma_start(w2_sb[:], w2.rearrange("(u p) v -> p u v", p=P))
                 load_block(c, k)
 
         def layer2(c, h_bf):

@@ -66,9 +66,11 @@ def tile_hiddenedgedistancemlp_b_kernel(tc, pocket, lig, w1, b1, w2, b2, offs, o
                 nc.sync.dma_start(windows[c * CHUNK // PAIRS][k][:], pocket[c * CHUNK // PAIRS, rows, :])
             nc.sync.dma_start(lig_sb[c][:, k, :], lig[rows, c * CHUNK : (c + 1) * CHUNK])
 
-        for k in range(CB):
-            load_block(0, k)
-            nc.sync.dma_start(w1_sb[:, k, :], w1[k * P : (k + 1) * P, :])
+        for k in range(CB + 1):
+            if k < CB:
+                load_block(0, k)
+            if k > 0:
+                nc.sync.dma_start(w1_sb[:, k - 1, :], w1[(k - 1) * P : k * P, :])
         for c in range(1, LOAD_AHEAD):
             for k in range(CB):
                 if c == 1 and k == DEFER:

@@ -28,7 +28,7 @@ def tile_hiddenedgedistancemlp_b_kernel(tc, pocket, lig, w1, b1, w2, b2, offs, o
     with (
         tc.tile_pool(name="held", bufs=1) as held,
         tc.tile_pool(name="lig_ring", bufs=LOAD_AHEAD + 1) as lig_ring,
-        tc.tile_pool(name="sum_ring", bufs=6) as sum_ring,
+        tc.tile_pool(name="sum_ring", bufs=3 * CB) as sum_ring,
         tc.tile_pool(name="rounded_ring", bufs=3) as rounded_ring,
         tc.tile_pool(name="hidden_ring", bufs=2) as hidden_ring,
         tc.tile_pool(name="out_ring", bufs=2 * VB) as out_ring,
@@ -103,7 +103,6 @@ def tile_hiddenedgedistancemlp_b_kernel(tc, pocket, lig, w1, b1, w2, b2, offs, o
             q = c * CHUNK // PAIRS
 
             h_ps = [psum1.tile([P, CHUNK], F32, name=f"h_ps{m}", tag="h_ps") for m in range(UB)]
-            step = PIECE if c == 0 else CHUNK
             kept = 0 if c == 0 else CLOSING
             closing = []
             for k in range(CB):
@@ -111,6 +110,7 @@ def tile_hiddenedgedistancemlp_b_kernel(tc, pocket, lig, w1, b1, w2, b2, offs, o
                     layer2(*waiting)
                 if c + LOAD_AHEAD < NCHUNKS:
                     load_block(c + LOAD_AHEAD, k)
+                step = PIECE if c == 0 or (c == 1 and k == 0) else CHUNK
                 for at in range(0, CHUNK, step):
                     s_f32 = sum_ring.tile([P, step], F32, name="s_f32")
                     for piece in range(step // PIECE):

@@ -30,6 +30,7 @@ def tile_hiddenedgedistancemlp_b_kernel(tc, pocket, lig, w1, b1, w2, b2, offs, o
         tc.tile_pool(name="lig_ring", bufs=LOAD_AHEAD + 1) as lig_ring,
         tc.tile_pool(name="sum_ring", bufs=3 * CB) as sum_ring,
         tc.tile_pool(name="rounded_ring", bufs=3) as rounded_ring,
+        tc.tile_pool(name="first_rounded", bufs=CB * CHUNK // PIECE) as first_rounded,
         tc.tile_pool(name="hidden_ring", bufs=2) as hidden_ring,
         tc.tile_pool(name="out_ring", bufs=2 * VB) as out_ring,
         tc.psum_pool(name="psum1", bufs=8 - VB) as psum1,
@@ -121,7 +122,7 @@ def tile_hiddenedgedistancemlp_b_kernel(tc, pocket, lig, w1, b1, w2, b2, offs, o
                             lig_sb[c][:, k, at + piece * PIECE : at + (piece + 1) * PIECE],
                             ADD,
                         )
-                    s_bf = rounded_ring.tile([P, step], BF16, name="s_bf")
+                    s_bf = (first_rounded if c == 0 else rounded_ring).tile([P, step], BF16, name="s_bf")
                     nc.scalar.copy(s_bf[:], s_f32[:])
                     if k >= CB - kept:
                         closing.append((k, s_bf))

import concourse.masks as masks
import concourse.mybir as mybir

F32 = mybir.dt.float32
BF16 = mybir.dt.bfloat16
U16 = mybir.dt.uint16
ADD = mybir.AluOpType.add
SILU = mybir.ActivationFunctionType.Silu

P = 128
B, C, S, N, D1, D2 = 2, 1024, 256, 4096, 512, 256
PAIRS = N // B
CB = C // P
UB = D1 // P
VB = D2 // P
CHUNK = 512
NCHUNKS = N // CHUNK
PIECE = S
LOAD_AHEAD = 3
CLOSING = 2
DEFER = 2

FLOPS = 2 * N * (C * D1 + D1 * D2)


def tile_hiddenedgedistancemlp_b_kernel(tc, pocket, lig, w1, b1, w2, b2, offs, out):
    nc = tc.nc
    with (
        tc.tile_pool(name="held", bufs=1) as held,
        tc.tile_pool(name="lig_ring", bufs=LOAD_AHEAD + 1) as lig_ring,
        tc.tile_pool(name="sum_ring", bufs=3 * CB) as sum_ring,
        tc.tile_pool(name="rounded_ring", bufs=3) as rounded_ring,
        tc.tile_pool(name="first_rounded", bufs=CB * CHUNK // PIECE) as first_rounded,
        tc.tile_pool(name="hidden_ring", bufs=2) as hidden_ring,
        tc.tile_pool(name="out_ring", bufs=2 * VB) as out_ring,
        tc.psum_pool(name="psum1", bufs=8 - VB) as psum1,
        tc.psum_pool(name="psum2", bufs=VB) as psum2,
    ):
        offsets = held.tile([P, N // 16], U16, name="offsets")
        nc.sync.dma_start(offsets[:], offs)

        warm = held.tile([P, 1], F32, name="warm")
        nc.gpsimd.memset(warm[:], 0.0)
        nc.scalar.activation(warm[:], warm[:], SILU)

        identity = held.tile([P, P], F32, name="identity")
        masks.make_identity(nc, identity[:])
        bias_rows = held.tile([P, P], F32, name="bias_rows")
        nc.gpsimd.memset(bias_rows[:], 0.0)
        nc.scalar.dma_start(bias_rows[0:UB, :], b1.rearrange("(m p) o -> m (p o)", p=P))
        nc.scalar.dma_start(bias_rows[UB : UB + VB, :], b2.rearrange("(v p) o -> v (p o)", p=P))
        bias_ps = psum2.tile([P, P], F32, name="bias_ps", tag="o_ps")
        nc.tensor.transpose(bias_ps[:], bias_rows[:], identity[:])
        bias_cols = held.tile([P, UB + VB], F32, name="bias_cols")
        nc.scalar.copy(bias_cols[:], bias_ps[:, 0 : UB + VB])

        windows = [[held.tile([P, S], F32, name=f"window{q}_{k}") for k in range(CB)] for q in range(B)]
        w1_sb = held.tile([P, CB, D1], BF16, name="w1_sb")
        w2_sb = held.tile([P, UB, D2], BF16, name="w2_sb")
        lig_sb = {}

        def load_block(c, k):
            rows = slice(k * P, (k + 1) * P)
            if k == 0:
                lig_sb[c] = lig_ring.tile([P, CB, CHUNK], F32, name="lig_sb")
            if c * CHUNK % PAIRS == 0:
                nc.sync.dma_start(windows[c * CHUNK // PAIRS][k][:], pocket[c * CHUNK // PAIRS, rows, :])
            nc.sync.dma_start(lig_sb[c][:, k, :], lig[rows, c * CHUNK : (c + 1) * CHUNK])

        for k in range(CB + 1):
            if k < CB:
                load_block(0, k)
            if k > 0:
                nc.sync.dma_start(w1_sb[:, k - 1, :], w1[(k - 1) * P : k * P, :])
        for c in range(1, LOAD_AHEAD):
            for k in range(CB):
                if c == 1 and k == DEFER:
                    nc.sync.dma_start(w2_sb[:], w2.rearrange("(u p) v -> p u v", p=P))
                load_block(c, k)

        def layer2(c, h_bf):
            last = c == NCHUNKS - 1
            span = CHUNK // 2 if last else CHUNK
            for at in range(0, CHUNK, span):
                for v in range(VB):
                    if last:
                        o_ps = psum1.tile([P, span], F32, name="o_ps_last", tag="h_ps")
                    else:
                        o_ps = psum2.tile([P, span], F32, name="o_ps")
                    for u in range(UB):
                        nc.tensor.matmul(
                            o_ps[:],
                            w2_sb[:, u, v * P : (v + 1) * P],
                            h_bf[:, u, at : at + span],
                            start=(u == 0),
                            stop=(u == UB - 1),
                        )
                    o_sb = out_ring.tile([P, span], F32, name="o_sb")
                    nc.scalar.activation(o_sb[:], o_ps[:], SILU, bias=bias_cols[:, UB + v : UB + v + 1])
                    nc.sync.dma_start(out[v * P : (v + 1) * P, c * CHUNK + at : c * CHUNK + at + span], o_sb[:])

        waiting = None
        for c in range(NCHUNKS):
            q = c * CHUNK // PAIRS

            h_ps = [psum1.tile([P, CHUNK], F32, name=f"h_ps{m}", tag="h_ps") for m in range(UB)]
            kept = 0 if c == 0 else CLOSING
            closing = []
            for k in range(CB):
                if k == DEFER and waiting is not None:
                    layer2(*waiting)
                if c + LOAD_AHEAD < NCHUNKS:
                    load_block(c + LOAD_AHEAD, k)
                step = PIECE if c == 0 or (c == 1 and k == 0) else CHUNK
                for at in range(0, CHUNK, step):
                    s_f32 = sum_ring.tile([P, step], F32, name="s_f32")
                    for piece in range(step // PIECE):
                        first = c * CHUNK + at + piece * PIECE
                        nc.vector.tensor_tensor(
                            s_f32[:, piece * PIECE : (piece + 1) * PIECE],
                            windows[q][k][:].indirect(offsets[:, first // 16 : (first + PIECE) // 16]),
                            lig_sb[c][:, k, at + piece * PIECE : at + (piece + 1) * PIECE],
                            ADD,
                        )
                    s_bf = (first_rounded if c == 0 else rounded_ring).tile([P, step], BF16, name="s_bf")
                    nc.scalar.copy(s_bf[:], s_f32[:])
                    if k >= CB - kept:
                        closing.append((k, s_bf))
                        continue
                    for m in range(UB):
                        nc.tensor.matmul(
                            h_ps[m][:, at : at + step],
                            w1_sb[:, k, m * P : (m + 1) * P],
                            s_bf[:],
                            start=(k == 0 and at == 0),
                            stop=(k == CB - 1 and at + step == CHUNK),
                        )
            for m in range(UB):
                for k, s_bf in closing:
                    nc.tensor.matmul(
                        h_ps[m][:],
                        w1_sb[:, k, m * P : (m + 1) * P],
                        s_bf[:],
                        start=False,
                        stop=(k == CB - 1),
                    )
            last = c == NCHUNKS - 1
            span = CHUNK // 2 if last else CHUNK
            h_bf = hidden_ring.tile([P, UB, CHUNK], BF16, name="h_bf")
            for at in range(0, CHUNK, span):
                for m in range(UB):
                    nc.scalar.activation(
                        h_bf[:, m, at : at + span], h_ps[m][:, at : at + span], SILU, bias=bias_cols[:, m : m + 1]
                    )
            waiting = (c, h_bf)
        layer2(*waiting)
